import numpy as np
import ml_dtypes


def mxq(x, axis, fmt="e4m3"):
    dtype, down = {"e4m3": (ml_dtypes.float8_e4m3fn, 7), "e5m2": (ml_dtypes.float8_e5m2, 14)}[fmt]
    v = np.moveaxis(np.asarray(x, np.float32).astype(ml_dtypes.bfloat16).astype(np.float64), axis, -1)
    blocks = v.reshape(v.shape[:-1] + (-1, 32))
    amax = np.abs(blocks).max(-1, keepdims=True)
    byte = np.maximum(np.where(amax > 0, np.frexp(amax)[1] - 1 + 127, 0) - down, 1)
    scale = np.exp2(byte - 127.0)
    codes = (blocks / scale).astype(np.float32).astype(dtype).astype(np.float64)
    return np.moveaxis((codes * scale).reshape(v.shape), -1, axis)


WIDE = False


def mx_kscale(k):
    if not WIDE:
        return np.ones(k)
    levels = np.array([10, -10, 5, -5, 0])
    if k % 512:
        return np.exp2(np.random.permutation(np.resize(levels, k // 32))).repeat(32)
    a = np.empty((k // 512, 16))
    for p in range(k // 512):
        a[p, :8] = np.random.permutation(np.resize(levels, 8))
        for g in range(8):
            far = levels[np.abs(levels - a[p, g]) >= 10]
            a[p, g + 8] = far[np.random.randint(len(far))]
    return np.exp2(a.ravel()).repeat(32)


BF16 = ml_dtypes.bfloat16


def bf(x):
    return np.asarray(x, np.float32).astype(BF16)


def f64(x):
    return np.asarray(x).astype(np.float64)


B, S, HID, H, KV, D = 1, 512, 2048, 16, 4, 128
EPS = 1e-6
THETA = 10000.0
HALF = D // 2


def rotate_half(x):
    return np.concatenate([-x[..., HALF:], x[..., :HALF]], axis=-1)


def rms_norm(x, w=None):
    n = x * (1.0 / np.sqrt(np.mean(x * x, axis=-1, keepdims=True) + EPS))
    return n if w is None else n * w


def draw0():
    s = mx_kscale(HID)
    c = 0.004 / np.sqrt(HID)
    inv_freq = 1.0 / THETA ** (np.arange(0, D, 2) / D)
    pos = np.random.randint(0, S) + np.arange(S)
    freqs = pos[:, None] * inv_freq[None, :]
    emb = np.concatenate([freqs, freqs], axis=-1)
    return {"hidden_states": bf(np.random.standard_normal((B, S, HID)) * s),
            "cos": bf(np.cos(emb)[None]),
            "sin": bf(np.sin(emb)[None]),
            "Wq": bf(np.random.standard_normal((H * D, HID)) * c / s[None, :]),
            "Wk": bf(np.random.standard_normal((KV * D, HID)) * c / s[None, :]),
            "Wv": bf(np.random.standard_normal((KV * D, HID)) * c / s[None, :]),
            "q_norm_w": bf(0.5 + 0.1 * np.random.standard_normal(D)),
            "k_norm_w": bf(0.5 + 0.1 * np.random.standard_normal(D))}


def core(hidden_states, cos, sin, Wq, Wk, Wv, q_norm_w, k_norm_w):
    xq = mxq(f64(hidden_states), 2, "e4m3")
    cs = f64(cos)[:, :, None, :]
    sn = f64(sin)[:, :, None, :]
    q = (xq @ mxq(f64(Wq).T, 0, "e4m3")).reshape(B, S, H, D)
    k = (xq @ mxq(f64(Wk).T, 0, "e4m3")).reshape(B, S, KV, D)
    v = (xq @ mxq(f64(Wv).T, 0, "e4m3")).reshape(B, S, KV, D)
    q = rms_norm(q, f64(q_norm_w))
    q = q * cs + rotate_half(q) * sn
    k = rms_norm(k, f64(k_norm_w))
    k = k * cs + rotate_half(k) * sn
    v = rms_norm(v)
    return q.transpose(0, 2, 1, 3), k.transpose(0, 2, 1, 3), v.transpose(0, 2, 1, 3)


def e4m3fn_bytes(y):
    return np.clip(np.asarray(y, np.float64), -448.0, 448.0).astype(np.float32).astype(ml_dtypes.float8_e4m3fn).view(np.uint8)


def e4m3fn_values(b):
    return np.asarray(b, np.uint8).view(ml_dtypes.float8_e4m3fn).astype(np.float64)


def setup_inputs():
    d = draw0()
    x0 = np.asarray(d['Wq']).astype(np.float64)
    s = (np.max(np.abs(x0), axis=(0,), keepdims=True) / 448.0).astype(np.float32)
    out = {}
    for k, v in d.items():
        if k == 'Wq':
            out['Wq_bytes'] = e4m3fn_bytes(x0 / s.astype(np.float64))
            out['Wq_scale'] = s
        else:
            out[k] = v
    return out


def reference(hidden_states, cos, sin, Wq_bytes, Wq_scale, Wk, Wv, q_norm_w, k_norm_w):
    return core(hidden_states, cos, sin, e4m3fn_values(Wq_bytes) * Wq_scale.astype(np.float64), Wk, Wv, q_norm_w, k_norm_w)

@@ -1,0 +1,329 @@
+from contextlib import ExitStack
+
+import concourse.mybir as mybir
+from concourse.masks import make_identity
+
+TOKENS, HID, D = 512, 2048, 128
+EPS = 1e-6
+FLOPS = 2 * TOKENS * HID * (2048 + 512 + 512)
+
+F32 = mybir.dt.float32
+BF16 = mybir.dt.bfloat16
+U32 = mybir.dt.uint32
+U8 = mybir.dt.uint8
+FP8 = mybir.dt.float8_e4m3fn
+FP8X4 = mybir.dt.float8_e4m3fn_x4
+ALU = mybir.AluOpType
+ACT = mybir.ActivationFunctionType
+
+P = 128
+HALF = D // 2
+
+SEQ = (("q", 0), ("k", 0), ("v", 0), ("q", 1), ("q", 2), ("q", 3))
+PRODUCTS = {
+    (-2, 0): ((0, 0),), (-2, 1): ((0, 1),), (-2, 2): ((0, 2),), (-2, 3): ((0, 3),),
+    (-1, 0): ((1, 0),), (-1, 1): ((1, 1),), (-1, 2): ((1, 2),),
+    (0, 0): ((1, 3), (2, 0)), (1, 0): ((2, 1), (2, 2)), (2, 0): ((2, 3),),
+    (2, 1): ((3, 0),), (2, 3): ((3, 1),), (3, 0): ((3, 2),), (3, 2): ((3, 3),),
+}
+GADDS = 2
+VCOPIES = ()
+MANUAL = True
+
+
+def tile_refattention_pa_kernel(
+    tc, hidden_states, cos, sin, Wq_bytes, Wq_scale, Wk, Wv, q_norm_w, k_norm_w, out_0, out_1, out_2
+):
+    nc = tc.nc
+    outs = {"q": out_0, "k": out_1, "v": out_2}
+    groups = len(SEQ)
+
+    with ExitStack() as ctx:
+        keep = ctx.enter_context(tc.tile_pool(name="keep", bufs=1))
+        rows = ctx.enter_context(tc.tile_pool(name="rows", bufs=16))
+        grp = ctx.enter_context(tc.tile_pool(name="grp", bufs=3))
+        cod = ctx.enter_context(tc.tile_pool(name="cod", bufs=2))
+        work = ctx.enter_context(tc.tile_pool(name="work", bufs=4))
+        stat = ctx.enter_context(tc.tile_pool(name="stat", bufs=3))
+        ps_t = ctx.enter_context(tc.psum_pool(name="ps_t", bufs=4))
+        ps_a = ctx.enter_context(tc.psum_pool(name="ps_a", bufs=4))
+
+        one = keep.tile([P, 1], F32, name="one")
+        nc.vector.memset(one[:], 1.0)
+        warm = keep.tile([P, 1], F32, name="warm")
+        nc.scalar.activation(out=warm[:], in_=one[:], func=ACT.Abs_reciprocal_sqrt)
+
+        ident = keep.tile([P, P], F32, name="ident")
+        make_identity(nc, ident[:])
+        ident_bf = keep.tile([P, P], BF16, name="ident_bf")
+        make_identity(nc, ident_bf[:])
+        diag = keep.tile([P, 2, 2, 2, D], BF16, name="diag")
+        nc.gpsimd.memset(diag[:], 0.0)
+
+        if MANUAL:
+            ctx.enter_context(tc.manual_schedule())
+
+        scl = keep.tile([P, HID], F32, name="scl")
+        scl_row = Wq_scale.rearrange("o k -> (o k)")
+        bytes_view = Wq_bytes.rearrange("(j t p) k -> j p t k", t=4, p=P)
+        wq8 = []
+        for j in range(4):
+            wq8.append(keep.tile([P, 4, HID], U8, name="wq8_%d" % j))
+        src = {("q", 0): [], ("q", 1): [], ("q", 2): [], ("q", 3): []}
+
+        def load_row(key, view, t):
+            r = rows.tile([P, HID], BF16, tag="row", name="%s%d_%d" % (key[0], key[1], t))
+            nc.sync.dma_start(out=r[:], in_=view[t])
+            src.setdefault(key, []).append(r)
+
+        def load_bytes(j, t0, t1):
+            nc.sync.dma_start(out=wq8[j][:, t0:t1, :], in_=bytes_view[j, :, t0:t1, :])
+
+        x_view = hidden_states.rearrange("b (t p) k -> (b t) p k", p=P)
+        k_view = Wk.rearrange("(t p) k -> t p k", p=P)
+        v_view = Wv.rearrange("(t p) k -> t p k", p=P)
+        def load_scales(c):
+            cols = slice(512 * c, 512 * (c + 1))
+            nc.sync.dma_start(out=scl[:, cols], in_=scl_row[cols].partition_broadcast(P))
+
+        load_scales(0)
+        for t in range(4):
+            load_bytes(0, t, t + 1)
+        for c in range(1, 4):
+            load_scales(c)
+            load_row(("x", 0), x_view, c - 1)
+        load_row(("x", 0), x_view, 3)
+        load_bytes(1, 0, 2)
+        cos_sb = keep.tile([P, 4, D], BF16, name="cos_sb")
+        sin_sw = keep.tile([P, 4, D], BF16, name="sin_sw")
+        sin_view = sin.rearrange("b (m p) d -> p (b m) d", p=P)
+        nc.sync.dma_start(out=cos_sb[:], in_=cos.rearrange("b (m p) d -> p (b m) d", p=P))
+        nc.sync.dma_start(out=sin_sw[:, :, 0:HALF], in_=sin_view[:, :, HALF:D])
+        nc.sync.dma_start(out=sin_sw[:, :, HALF:D], in_=sin_view[:, :, 0:HALF])
+        gain = keep.tile([P, 2, D], BF16, name="gain")
+        nc.sync.dma_start(out=gain[:, 0, :], in_=q_norm_w.partition_broadcast(P))
+        nc.sync.dma_start(out=gain[:, 1, :], in_=k_norm_w.partition_broadcast(P))
+        load_bytes(1, 2, 4)
+        for t in range(4):
+            load_row(("k", 0), k_view, t)
+        load_bytes(2, 0, 4)
+        for t in range(4):
+            load_row(("v", 0), v_view, t)
+        load_bytes(3, 0, 4)
+
+        cf_all = keep.tile([P, 2, 4, 2, D], F32, name="cf_all")
+        cf = {"q": cf_all[:, 0, :, :, :], "k": cf_all[:, 1, :, :, :]}
+
+        def tables():
+            g_t = ps_t.tile([P, 2, P], BF16, tag="tp", name="g_t")
+            for kind in range(2):
+                nc.tensor.transpose(g_t[:, kind, :], gain[:, kind, :], ident_bf[:])
+            wcol = keep.tile([P, 2, 2], F32, name="wcol")
+            nc.scalar.copy(out=wcol[:, :, 0:1], in_=g_t[:, :, 0:1])
+            nc.scalar.activation(out=wcol[:, :, 1:2], in_=g_t[:, :, 0:1], func=ACT.Copy, scale=-1.0)
+            turned = []
+            for name, table in (("cos_t", cos_sb), ("sin_t", sin_sw)):
+                tt = ps_t.tile([P, 4, P], BF16, tag="tp", name=name + "_ps")
+                for m in range(4):
+                    nc.tensor.transpose(tt[:, m, :], table[:, m, :], ident_bf[:])
+                sb = keep.tile([P, 4, P], BF16, name=name)
+                nc.scalar.copy(out=sb[:], in_=tt[:])
+                turned.append(sb)
+            lo, hi = slice(0, HALF), slice(HALF, P)
+            for kind in range(2):
+                for part, source, o, sign in ((lo, 0, 0, 0), (hi, 0, 1, 0), (lo, 1, 1, 0), (hi, 1, 0, 1)):
+                    nc.scalar.activation(
+                        out=diag[part, kind, source, o, :], in_=ident_bf[part, :], func=ACT.Copy,
+                        scale=wcol[part, kind, sign : sign + 1],
+                    )
+            for kind in range(2):
+                for half in range(2):
+                    tb = ps_t.tile([P, 2, 2, D], F32, tag="tp", name="tab_%d_%d" % (kind, half))
+                    for mm in range(2):
+                        for source in range(2):
+                            nc.tensor.matmul(
+                                out=tb[:, mm, :, :], lhsT=turned[source][:, 2 * half + mm, :],
+                                rhs=diag[:, kind, source, :, :], start=(source == 0), stop=(source == 1),
+                            )
+                    nc.scalar.copy(out=cf_all[:, kind, 2 * half : 2 * half + 2, :, :], in_=tb[:])
+
+        grouped = {}
+        codes = {}
+        planes = {}
+        acc = {}
+        ssq = {}
+        inv = {}
+        prod = {}
+        rot = {}
+
+        def product_piece(j, t, cols):
+            nc.vector.tensor_tensor(
+                out=src[("q", j)][t][:, cols], in0=wq8[j][:, t, cols].bitcast(FP8), in1=scl[:, cols], op=ALU.mult
+            )
+
+        def product(j, t):
+            src[("q", j)].append(rows.tile([P, HID], BF16, tag="row", name="q%d_%d" % (j, t)))
+            product_piece(j, t, slice(0, HID))
+
+        def turn(key, t, halves=(0, 1)):
+            if key not in grouped:
+                grouped[key] = grp.tile([P, 4, 512, 4], BF16, tag="grp", name="grp_%s%d" % key, align_bytes=64)
+            words = src[key][t][:].bitcast(F32)
+            gw = grouped[key][:].bitcast(F32)
+            for half in halves:
+                tp = ps_t.tile([P, 2, 2, P], F32, tag="tp", name="tp_%s%d_%d_%d" % (key[0], key[1], t, half))
+                for gg in range(2):
+                    g = 2 * half + gg
+                    for u in range(2):
+                        nc.tensor.transpose(tp[:, gg, u, :], words[:, 256 * g + u : 256 * (g + 1) : 2], ident[:])
+                dst = gw[:, 2 * half : 2 * half + 2, t * P : (t + 1) * P, :]
+                if half == 1 and key in VCOPIES:
+                    nc.vector.tensor_copy(out=dst, in_=tp[:].rearrange("p g u r -> p g r u"))
+                else:
+                    nc.scalar.copy(out=dst, in_=tp[:].rearrange("p g u r -> p g r u"))
+
+        def quantise(key, half):
+            if half == 0:
+                pool = keep if key[0] == "x" else cod
+                codes[key] = pool.tile([P, 4, 512], U32, tag="codes_" + ("x" if key[0] == "x" else "w"),
+                                       name="codes_%s%d" % key, align_bytes=64)
+                planes[key] = pool.tile([P, 4, 512], U8, tag="planes_" + ("x" if key[0] == "x" else "w"),
+                                        name="planes_%s%d" % key, align_bytes=64)
+            gs = slice(2 * half, 2 * half + 2)
+            nc.vector.quantize_mx(
+                out=codes[key][:, gs, :].rearrange("p g c -> p (g c)").bitcast(FP8X4),
+                scales=planes[key][:, gs, :].rearrange("p g c -> p (g c)"),
+                in_=grouped[key][:, gs, :, :].rearrange("p g r t -> p (g r t)"),
+            )
+
+        def multiply(r, m):
+            key = SEQ[r]
+            a = ps_a.tile([P, 512], F32, tag="acc", name="acc_%d_%d" % (r, m))
+            toks = slice(m * P, (m + 1) * P)
+            for g in range(4):
+                nc.tensor.matmul_mx(
+                    out=a[:],
+                    lhsT=codes[("x", 0)][:, g, toks].bitcast(FP8X4),
+                    lhsT_scale=planes[("x", 0)][:, g, toks],
+                    rhs=codes[key][:, g, :].bitcast(FP8X4),
+                    rhs_scale=planes[key][:, g, :],
+                    start=(g == 0),
+                    stop=(g == 3),
+                )
+            acc[(r, m)] = a
+
+        def squares(r, m):
+            if m == 0:
+                ssq[r] = stat.tile([P, 16], F32, tag="ssq", name="ssq_%d" % r)
+            for h in range(4):
+                junk = work.tile([P, D], F32, tag="junk", name="junk_%d_%d_%d" % (r, m, h))
+                nc.scalar.activation(
+                    out=junk[:], in_=acc[(r, m)][:, h * D : (h + 1) * D], func=ACT.Square,
+                    accum_out=ssq[r][:, 4 * m + h : 4 * m + h + 1],
+                )
+
+        def root(r):
+            inv[r] = stat.tile([P, 16], F32, tag="inv", name="inv_%d" % r)
+            nc.scalar.activation(out=inv[r][:], in_=ssq[r][:], func=ACT.Abs_reciprocal_sqrt, scale=1.0 / D, bias=EPS)
+
+        def rope_mult(r, m):
+            pr = work.tile([P, 4, 2, D], F32, tag="prod", name="prod_%d_%d" % (r, m))
+            nc.vector.tensor_tensor(
+                out=pr[:],
+                in0=acc[(r, m)][:].rearrange("p (h d) -> p h d", h=4).unsqueeze(2).to_broadcast([P, 4, 2, D]),
+                in1=cf[SEQ[r][0]][:, m, :, :].unsqueeze(1).to_broadcast([P, 4, 2, D]),
+                op=ALU.mult,
+            )
+            prod[(r, m)] = pr
+
+        def rope_mult_scaled(r, m):
+            pr = work.tile([P, 4, 2, D], F32, tag="prod", name="prod_%d_%d" % (r, m))
+            for h in range(4):
+                nc.vector.scalar_tensor_tensor(
+                    out=pr[:, h, :, :],
+                    in0=acc[(r, m)][:, h * D : (h + 1) * D].unsqueeze(1).to_broadcast([P, 2, D]),
+                    scalar=inv[r][:, 4 * m + h : 4 * m + h + 1],
+                    in1=cf[SEQ[r][0]][:, m, :, :],
+                    op0=ALU.mult, op1=ALU.mult,
+                )
+            prod[(r, m)] = pr
+
+        def store_only(r, m):
+            key = SEQ[r]
+            h0 = 4 * key[1]
+            dst = outs[key[0]][0, h0 : h0 + 4, m * P : (m + 1) * P, :].rearrange("h s d -> s h d")
+            nc.sync.dma_start(out=dst, in_=rot[(r, m)][:].rearrange("p h a b -> p h (a b)"))
+
+        def rope_add(r, m, eng):
+            ro = work.tile([P, 4, 2, HALF], F32, tag="rot", bufs=5, name="rot_%d_%d" % (r, m))
+            pr = prod[(r, m)]
+            eng.tensor_tensor(out=ro[:], in0=pr[:, :, :, 0:HALF], in1=pr[:, :, :, HALF:D], op=ALU.add)
+            rot[(r, m)] = ro
+
+        def finish(r, m):
+            key = SEQ[r]
+            o = work.tile([P, 4, D], F32, tag="o", bufs=6, name="o_%d_%d" % (r, m))
+            for h in range(4):
+                if key[0] == "v":
+                    val = acc[(r, m)][:, h * D : (h + 1) * D]
+                else:
+                    val = rot[(r, m)][:, h, :, :].rearrange("p a b -> p (a b)")
+                nc.scalar.activation(out=o[:, h, :], in_=val, func=ACT.Copy, scale=inv[r][:, 4 * m + h : 4 * m + h + 1])
+            h0 = 4 * key[1]
+            dst = outs[key[0]][0, h0 : h0 + 4, m * P : (m + 1) * P, :].rearrange("h s d -> s h d")
+            nc.sync.dma_start(out=dst, in_=o[:])
+
+        for r in range(-2, groups + 1):
+            live = 0 <= r < groups
+            is_v = live and SEQ[r][0] == "v"
+            if r == -1:
+                tables()
+            if r == -2:
+                for t in range(4):
+                    src[("q", 0)].append(rows.tile([P, HID], BF16, tag="row", name="q0_%d" % t))
+                for half in range(2):
+                    for c in (2 * half, 2 * half + 1):
+                        for t in range(4):
+                            product_piece(0, t, slice(512 * c, 512 * (c + 1)))
+                    for t in ((0,), (1, 2, 3))[half]:
+                        turn(("x", 0), t)
+                    for t in range(4):
+                        turn(("q", 0), t, (half,))
+            for m in range(4 if r > -2 else 0):
+                if live:
+                    multiply(r, m)
+                    squares(r, m)
+                if r == groups and m >= 2:
+                    if m == 2:
+                        store_only(r - 1, 3)
+                        finish(r - 1, 2)
+                elif 1 <= r and SEQ[r - 1][0] != "v":
+                    finish(r - 1, m)
+                for jt in PRODUCTS.get((r, m), ()):
+                    product(jt[0], jt[1])
+                if r == -2:
+                    turn(("x", 0), m)
+                if 0 <= r + 2 < groups:
+                    turn(SEQ[r + 2], m)
+            if live:
+                root(r)
+            if is_v:
+                for m in range(4):
+                    finish(r, m)
+            if r == -1:
+                quantise(("x", 0), 0)
+                quantise(("x", 0), 1)
+            if 0 <= r + 1 < groups:
+                quantise(SEQ[r + 1], 0)
+                quantise(SEQ[r + 1], 1)
+            if live and not is_v:
+                for m in range(4):
+                    if r == groups - 1 and m == 3:
+                        rope_mult_scaled(r, m)
+                    else:
+                        rope_mult(r, m)
+                    if m >= 1 and m - 1 < GADDS:
+                        rope_add(r, m - 1, nc.gpsimd)
+                for m in range(4):
+                    if m >= GADDS:
+                        rope_add(r, m, nc.vector)

@@ -41,6 +41,7 @@ def tile_refattention_pa_kernel(
     with ExitStack() as ctx:
         keep = ctx.enter_context(tc.tile_pool(name="keep", bufs=1))
         rows = ctx.enter_context(tc.tile_pool(name="rows", bufs=16))
+        raw = ctx.enter_context(tc.tile_pool(name="raw", bufs=3))
         grp = ctx.enter_context(tc.tile_pool(name="grp", bufs=3))
         cod = ctx.enter_context(tc.tile_pool(name="cod", bufs=2))
         work = ctx.enter_context(tc.tile_pool(name="work", bufs=4))
@@ -66,9 +67,7 @@ def tile_refattention_pa_kernel(
         scl = keep.tile([P, HID], F32, name="scl")
         scl_row = Wq_scale.rearrange("o k -> (o k)")
         bytes_view = Wq_bytes.rearrange("(j t p) k -> j p t k", t=4, p=P)
-        wq8 = []
-        for j in range(4):
-            wq8.append(keep.tile([P, 4, HID], U8, name="wq8_%d" % j))
+        wq8 = {}
         src = {("q", 0): [], ("q", 1): [], ("q", 2): [], ("q", 3): []}
 
         def load_row(key, view, t):
@@ -77,6 +76,8 @@ def tile_refattention_pa_kernel(
             src.setdefault(key, []).append(r)
 
         def load_bytes(j, t0, t1):
+            if j not in wq8:
+                wq8[j] = raw.tile([P, 4, HID], U8, tag="wq8", name="wq8_%d" % j)
             nc.sync.dma_start(out=wq8[j][:, t0:t1, :], in_=bytes_view[j, :, t0:t1, :])
 
         x_view = hidden_states.rearrange("b (t p) k -> (b t) p k", p=P)
@@ -227,7 +228,7 @@ def tile_refattention_pa_kernel(
             nc.scalar.activation(out=inv[r][:], in_=ssq[r][:], func=ACT.Abs_reciprocal_sqrt, scale=1.0 / D, bias=EPS)
 
         def rope_mult(r, m):
-            pr = work.tile([P, 4, 2, D], F32, tag="prod", name="prod_%d_%d" % (r, m))
+            pr = work.tile([P, 4, 2, D], F32, tag="prod", bufs=5, name="prod_%d_%d" % (r, m))
             nc.vector.tensor_tensor(
                 out=pr[:],
                 in0=acc[(r, m)][:].rearrange("p (h d) -> p h d", h=4).unsqueeze(2).to_broadcast([P, 4, 2, D]),
@@ -237,7 +238,7 @@ def tile_refattention_pa_kernel(
             prod[(r, m)] = pr
 
         def rope_mult_scaled(r, m):
-            pr = work.tile([P, 4, 2, D], F32, tag="prod", name="prod_%d_%d" % (r, m))
+            pr = work.tile([P, 4, 2, D], F32, tag="prod", bufs=5, name="prod_%d_%d" % (r, m))
             for h in range(4):
                 nc.vector.scalar_tensor_tensor(
                     out=pr[:, h, :, :],
@@ -255,10 +256,16 @@ def tile_refattention_pa_kernel(
             nc.sync.dma_start(out=dst, in_=rot[(r, m)][:].rearrange("p h a b -> p h (a b)"))
 
         def rope_add(r, m, eng):
-            ro = work.tile([P, 4, 2, HALF], F32, tag="rot", bufs=5, name="rot_%d_%d" % (r, m))
+            kept = m == 3 and r < groups - 1
+            ro = work.tile([P, 4, 2, HALF], F32, tag="rotl" if kept else "rot", bufs=2 if kept else 5, name="rot_%d_%d" % (r, m))
             pr = prod[(r, m)]
             eng.tensor_tensor(out=ro[:], in0=pr[:, :, :, 0:HALF], in1=pr[:, :, :, HALF:D], op=ALU.add)
             rot[(r, m)] = ro
+
+        gate = keep.tile([P, 8], U32, name="gate")
+
+        def wait_for_quantise(key):
+            nc.gpsimd.tensor_copy(out=gate[:], in_=codes[key][:, 3, 504:512])
 
         def finish(r, m):
             key = SEQ[r]
@@ -273,6 +280,8 @@ def tile_refattention_pa_kernel(
             dst = outs[key[0]][0, h0 : h0 + 4, m * P : (m + 1) * P, :].rearrange("h s d -> s h d")
             nc.sync.dma_start(out=dst, in_=o[:])
 
+        left = []
+        late = []
         for r in range(-2, groups + 1):
             live = 0 <= r < groups
             is_v = live and SEQ[r][0] == "v"
@@ -297,8 +306,10 @@ def tile_refattention_pa_kernel(
                     if m == 2:
                         store_only(r - 1, 3)
                         finish(r - 1, 2)
-                elif 1 <= r and SEQ[r - 1][0] != "v":
+                elif 1 <= r and SEQ[r - 1][0] != "v" and not (m == 3 and r - 1 < groups - 1):
                     finish(r - 1, m)
+                if m == (0 if r == groups else 3) and late:
+                    finish(late.pop(), 3)
                 for jt in PRODUCTS.get((r, m), ()):
                     product(jt[0], jt[1])
                 if r == -2:
@@ -317,13 +328,21 @@ def tile_refattention_pa_kernel(
                 quantise(SEQ[r + 1], 0)
                 quantise(SEQ[r + 1], 1)
             if live and not is_v:
+                last = r == groups - 1
+                if left:
+                    if not last:
+                        wait_for_quantise(SEQ[r + 1])
+                    rope_add(left[0], 3, nc.gpsimd)
+                    late.append(left.pop())
                 for m in range(4):
-                    if r == groups - 1 and m == 3:
+                    if last and m == 3:
                         rope_mult_scaled(r, m)
                     else:
                         rope_mult(r, m)
                     if m >= 1 and m - 1 < GADDS:
                         rope_add(r, m - 1, nc.gpsimd)
-                for m in range(4):
-                    if m >= GADDS:
-                        rope_add(r, m, nc.vector)
+                rope_add(r, 2, nc.vector)
+                if last:
+                    rope_add(r, 3, nc.vector)
+                else:
+                    left.append(r)

@@ -23,7 +23,7 @@ SEQ = (("q", 0), ("k", 0), ("v", 0), ("q", 1), ("q", 2), ("q", 3))
 PRODUCTS = {
     (-2, 0): ((0, 0),), (-2, 1): ((0, 1),), (-2, 2): ((0, 2),), (-2, 3): ((0, 3),),
     (-1, 0): ((1, 0),), (-1, 1): ((1, 1),), (-1, 2): ((1, 2),),
-    (0, 0): ((1, 3), (2, 0)), (1, 0): ((2, 1), (2, 2)), (2, 0): ((2, 3),),
+    (0, 0): ((1, 3), (2, 0), (2, 1)), (1, 0): ((2, 2),), (2, 0): ((2, 3),),
     (2, 1): ((3, 0),), (2, 3): ((3, 1),), (3, 0): ((3, 2),), (3, 2): ((3, 3),),
 }
 GADDS = 2
@@ -54,6 +54,11 @@ def tile_refattention_pa_kernel(
         warm = keep.tile([P, 1], F32, name="warm")
         nc.scalar.activation(out=warm[:], in_=one[:], func=ACT.Abs_reciprocal_sqrt)
 
+        spread = grp.tile([P, HID - 1024], F32, tag="grp", name="spread", align_bytes=64)
+        nc.gpsimd.memset(spread[:], 0.0)
+        ones = keep.tile([P, P], F32, name="ones")
+        nc.vector.memset(ones[:], 1.0)
+
         ident = keep.tile([P, P], F32, name="ident")
         make_identity(nc, ident[:])
         ident_bf = keep.tile([P, P], BF16, name="ident_bf")
@@ -75,10 +80,10 @@ def tile_refattention_pa_kernel(
             nc.sync.dma_start(out=r[:], in_=view[t])
             src.setdefault(key, []).append(r)
 
-        def load_bytes(j, t0, t1):
+        def load_bytes(j, t0, t1, cols=slice(0, HID)):
             if j not in wq8:
                 wq8[j] = raw.tile([P, 4, HID], U8, tag="wq8", name="wq8_%d" % j)
-            nc.sync.dma_start(out=wq8[j][:, t0:t1, :], in_=bytes_view[j, :, t0:t1, :])
+            nc.sync.dma_start(out=wq8[j][:, t0:t1, cols], in_=bytes_view[j, :, t0:t1, cols])
 
         x_view = hidden_states.rearrange("b (t p) k -> (b t) p k", p=P)
         k_view = Wk.rearrange("(t p) k -> t p k", p=P)
@@ -89,11 +94,17 @@ def tile_refattention_pa_kernel(
 
         load_scales(0)
         for t in range(4):
-            load_bytes(0, t, t + 1)
-        for c in range(1, 4):
-            load_scales(c)
-            load_row(("x", 0), x_view, c - 1)
-        load_row(("x", 0), x_view, 3)
+            load_bytes(0, t, t + 1, slice(0, 512))
+        nc.sync.dma_start(out=spread[0:1, :], in_=Wq_scale[:, 1024:HID])
+        load_scales(1)
+        for t in range(4):
+            load_bytes(0, t, t + 1, slice(512, HID))
+        for c in range(2):
+            sp = ps_a.tile([P, 512], F32, tag="acc", name="sp_%d" % c)
+            nc.tensor.matmul(out=sp[:], lhsT=ones[:], rhs=spread[:, 512 * c : 512 * (c + 1)], start=True, stop=True)
+            nc.scalar.copy(out=scl[:, 512 * (c + 2) : 512 * (c + 3)], in_=sp[:])
+        for t in range(4):
+            load_row(("x", 0), x_view, t)
         load_bytes(1, 0, 2)
         cos_sb = keep.tile([P, 4, D], BF16, name="cos_sb")
         sin_sw = keep.tile([P, 4, D], BF16, name="sin_sw")
@@ -228,7 +239,8 @@ def tile_refattention_pa_kernel(
             nc.scalar.activation(out=inv[r][:], in_=ssq[r][:], func=ACT.Abs_reciprocal_sqrt, scale=1.0 / D, bias=EPS)
 
         def rope_mult(r, m):
-            pr = work.tile([P, 4, 2, D], F32, tag="prod", bufs=5, name="prod_%d_%d" % (r, m))
+            pe = m == 2 and r in (1, 3)
+            pr = work.tile([P, 4, 2, D], F32, tag="prodp" if pe else "prod", bufs=1 if pe else 4, name="prod_%d_%d" % (r, m))
             nc.vector.tensor_tensor(
                 out=pr[:],
                 in0=acc[(r, m)][:].rearrange("p (h d) -> p h d", h=4).unsqueeze(2).to_broadcast([P, 4, 2, D]),
@@ -238,7 +250,8 @@ def tile_refattention_pa_kernel(
             prod[(r, m)] = pr
 
         def rope_mult_scaled(r, m):
-            pr = work.tile([P, 4, 2, D], F32, tag="prod", bufs=5, name="prod_%d_%d" % (r, m))
+            pe = m == 2 and r in (1, 3)
+            pr = work.tile([P, 4, 2, D], F32, tag="prodp" if pe else "prod", bufs=1 if pe else 4, name="prod_%d_%d" % (r, m))
             for h in range(4):
                 nc.vector.scalar_tensor_tensor(
                     out=pr[:, h, :, :],
@@ -267,11 +280,29 @@ def tile_refattention_pa_kernel(
         def wait_for_quantise(key):
             nc.gpsimd.tensor_copy(out=gate[:], in_=codes[key][:, 3, 504:512])
 
+        def pe_add(r, m):
+            s = ps_t.tile([P, 512], F32, tag="tp", name="sum_%d_%d" % (r, m))
+            pr = prod[(r, m)]
+            for half in range(2):
+                nc.tensor.matmul(
+                    out=s[:].rearrange("p (h d) -> p h d", d=HALF), lhsT=ident[:],
+                    rhs=pr[:, :, :, half * HALF : (half + 1) * HALF].rearrange("p h a d -> p (h a) d"),
+                    start=(half == 0), stop=(half == 1),
+                )
+            summed[(r, m)] = s
+
+        summed = {}
+
         def finish(r, m):
             key = SEQ[r]
+            if key[0] != "v" and m in (3,):
+                store_only(r, m)
+                return
             o = work.tile([P, 4, D], F32, tag="o", bufs=6, name="o_%d_%d" % (r, m))
             for h in range(4):
-                if key[0] == "v":
+                if (r, m) in summed:
+                    val = summed[(r, m)][:, h * D : (h + 1) * D]
+                elif key[0] == "v":
                     val = acc[(r, m)][:, h * D : (h + 1) * D]
                 else:
                     val = rot[(r, m)][:, h, :, :].rearrange("p a b -> p (a b)")
@@ -298,15 +329,20 @@ def tile_refattention_pa_kernel(
                         turn(("x", 0), t)
                     for t in range(4):
                         turn(("q", 0), t, (half,))
+            if r - 2 in (1, 3):
+                pe_add(r - 2, 2)
+                finish(r - 2, 2)
             for m in range(4 if r > -2 else 0):
                 if live:
                     multiply(r, m)
                     squares(r, m)
+                    if m == 3:
+                        root(r)
                 if r == groups and m >= 2:
                     if m == 2:
                         store_only(r - 1, 3)
                         finish(r - 1, 2)
-                elif 1 <= r and SEQ[r - 1][0] != "v" and not (m == 3 and r - 1 < groups - 1):
+                elif 1 <= r and SEQ[r - 1][0] != "v" and not (m == 3 and r - 1 < groups - 1) and not (m == 2 and r - 1 in (1, 3)):
                     finish(r - 1, m)
                 if m == (0 if r == groups else 3) and late:
                     finish(late.pop(), 3)
@@ -316,8 +352,6 @@ def tile_refattention_pa_kernel(
                     turn(("x", 0), m)
                 if 0 <= r + 2 < groups:
                     turn(SEQ[r + 2], m)
-            if live:
-                root(r)
             if is_v:
                 for m in range(4):
                     finish(r, m)
@@ -335,13 +369,14 @@ def tile_refattention_pa_kernel(
                     rope_add(left[0], 3, nc.gpsimd)
                     late.append(left.pop())
                 for m in range(4):
-                    if last and m == 3:
+                    if m in (3,) or (last and m == 3):
                         rope_mult_scaled(r, m)
                     else:
                         rope_mult(r, m)
                     if m >= 1 and m - 1 < GADDS:
                         rope_add(r, m - 1, nc.gpsimd)
-                rope_add(r, 2, nc.vector)
+                if r not in (1, 3):
+                    rope_add(r, 2, nc.vector)
                 if last:
                     rope_add(r, 3, nc.vector)
                 else:

from contextlib import ExitStack

import concourse.mybir as mybir
from concourse.masks import make_identity

TOKENS, HID, D = 512, 2048, 128
EPS = 1e-6
FLOPS = 2 * TOKENS * HID * (2048 + 512 + 512)

F32 = mybir.dt.float32
BF16 = mybir.dt.bfloat16
U32 = mybir.dt.uint32
U8 = mybir.dt.uint8
FP8 = mybir.dt.float8_e4m3fn
FP8X4 = mybir.dt.float8_e4m3fn_x4
ALU = mybir.AluOpType
ACT = mybir.ActivationFunctionType

P = 128
HALF = D // 2

SEQ = (("q", 0), ("k", 0), ("v", 0), ("q", 1), ("q", 2), ("q", 3))
PRODUCTS = {
    (-2, 0): ((0, 0),), (-2, 1): ((0, 1),), (-2, 2): ((0, 2),), (-2, 3): ((0, 3),),
    (-1, 0): ((1, 0),), (-1, 1): ((1, 1),), (-1, 2): ((1, 2),),
    (0, 0): ((1, 3), (2, 0), (2, 1)), (1, 0): ((2, 2),), (2, 0): ((2, 3),),
    (2, 1): ((3, 0),), (2, 3): ((3, 1),), (3, 0): ((3, 2),), (3, 2): ((3, 3),),
}
GADDS = 2
VCOPIES = ()
MANUAL = True


def tile_refattention_pa_kernel(
    tc, hidden_states, cos, sin, Wq_bytes, Wq_scale, Wk, Wv, q_norm_w, k_norm_w, out_0, out_1, out_2
):
    nc = tc.nc
    outs = {"q": out_0, "k": out_1, "v": out_2}
    groups = len(SEQ)

    with ExitStack() as ctx:
        keep = ctx.enter_context(tc.tile_pool(name="keep", bufs=1))
        rows = ctx.enter_context(tc.tile_pool(name="rows", bufs=16))
        raw = ctx.enter_context(tc.tile_pool(name="raw", bufs=3))
        grp = ctx.enter_context(tc.tile_pool(name="grp", bufs=3))
        cod = ctx.enter_context(tc.tile_pool(name="cod", bufs=2))
        work = ctx.enter_context(tc.tile_pool(name="work", bufs=4))
        stat = ctx.enter_context(tc.tile_pool(name="stat", bufs=3))
        ps_t = ctx.enter_context(tc.psum_pool(name="ps_t", bufs=4))
        ps_a = ctx.enter_context(tc.psum_pool(name="ps_a", bufs=4))

        one = keep.tile([P, 1], F32, name="one")
        nc.vector.memset(one[:], 1.0)
        warm = keep.tile([P, 1], F32, name="warm")
        nc.scalar.activation(out=warm[:], in_=one[:], func=ACT.Abs_reciprocal_sqrt)

        spread = grp.tile([P, HID - 1024], F32, tag="grp", name="spread", align_bytes=64)
        nc.gpsimd.memset(spread[:], 0.0)
        ones = keep.tile([P, P], F32, name="ones")
        nc.vector.memset(ones[:], 1.0)

        ident = keep.tile([P, P], F32, name="ident")
        make_identity(nc, ident[:])
        ident_bf = keep.tile([P, P], BF16, name="ident_bf")
        make_identity(nc, ident_bf[:])
        diag = keep.tile([P, 2, 2, 2, D], BF16, name="diag")
        nc.gpsimd.memset(diag[:], 0.0)

        if MANUAL:
            ctx.enter_context(tc.manual_schedule())

        scl = keep.tile([P, HID], F32, name="scl")
        scl_row = Wq_scale.rearrange("o k -> (o k)")
        bytes_view = Wq_bytes.rearrange("(j t p) k -> j p t k", t=4, p=P)
        wq8 = {}
        src = {("q", 0): [], ("q", 1): [], ("q", 2): [], ("q", 3): []}

        def load_row(key, view, t):
            r = rows.tile([P, HID], BF16, tag="row", name="%s%d_%d" % (key[0], key[1], t))
            nc.sync.dma_start(out=r[:], in_=view[t])
            src.setdefault(key, []).append(r)

        def load_bytes(j, t0, t1, cols=slice(0, HID)):
            if j not in wq8:
                wq8[j] = raw.tile([P, 4, HID], U8, tag="wq8", name="wq8_%d" % j)
            nc.sync.dma_start(out=wq8[j][:, t0:t1, cols], in_=bytes_view[j, :, t0:t1, cols])

        x_view = hidden_states.rearrange("b (t p) k -> (b t) p k", p=P)
        k_view = Wk.rearrange("(t p) k -> t p k", p=P)
        v_view = Wv.rearrange("(t p) k -> t p k", p=P)
        def load_scales(c):
            cols = slice(512 * c, 512 * (c + 1))
            nc.sync.dma_start(out=scl[:, cols], in_=scl_row[cols].partition_broadcast(P))

        load_scales(0)
        for t in range(4):
            load_bytes(0, t, t + 1, slice(0, 512))
        nc.sync.dma_start(out=spread[0:1, :], in_=Wq_scale[:, 1024:HID])
        load_scales(1)
        for t in range(4):
            load_bytes(0, t, t + 1, slice(512, HID))
        for c in range(2):
            sp = ps_a.tile([P, 512], F32, tag="acc", name="sp_%d" % c)
            nc.tensor.matmul(out=sp[:], lhsT=ones[:], rhs=spread[:, 512 * c : 512 * (c + 1)], start=True, stop=True)
            nc.scalar.copy(out=scl[:, 512 * (c + 2) : 512 * (c + 3)], in_=sp[:])
        for t in range(4):
            load_row(("x", 0), x_view, t)
        load_bytes(1, 0, 2)
        cos_sb = keep.tile([P, 4, D], BF16, name="cos_sb")
        sin_sw = keep.tile([P, 4, D], BF16, name="sin_sw")
        sin_view = sin.rearrange("b (m p) d -> p (b m) d", p=P)
        nc.sync.dma_start(out=cos_sb[:], in_=cos.rearrange("b (m p) d -> p (b m) d", p=P))
        nc.sync.dma_start(out=sin_sw[:, :, 0:HALF], in_=sin_view[:, :, HALF:D])
        nc.sync.dma_start(out=sin_sw[:, :, HALF:D], in_=sin_view[:, :, 0:HALF])
        gain = keep.tile([P, 2, D], BF16, name="gain")
        nc.sync.dma_start(out=gain[:, 0, :], in_=q_norm_w.partition_broadcast(P))
        nc.sync.dma_start(out=gain[:, 1, :], in_=k_norm_w.partition_broadcast(P))
        load_bytes(1, 2, 4)
        for t in range(4):
            load_row(("k", 0), k_view, t)
        load_bytes(2, 0, 4)
        for t in range(4):
            load_row(("v", 0), v_view, t)
        load_bytes(3, 0, 4)

        cf_all = keep.tile([P, 2, 4, 2, D], F32, name="cf_all")
        cf = {"q": cf_all[:, 0, :, :, :], "k": cf_all[:, 1, :, :, :]}

        def tables():
            g_t = ps_t.tile([P, 2, P], BF16, tag="tp", name="g_t")
            for kind in range(2):
                nc.tensor.transpose(g_t[:, kind, :], gain[:, kind, :], ident_bf[:])
            wcol = keep.tile([P, 2, 2], F32, name="wcol")
            nc.scalar.copy(out=wcol[:, :, 0:1], in_=g_t[:, :, 0:1])
            nc.scalar.activation(out=wcol[:, :, 1:2], in_=g_t[:, :, 0:1], func=ACT.Copy, scale=-1.0)
            turned = []
            for name, table in (("cos_t", cos_sb), ("sin_t", sin_sw)):
                tt = ps_t.tile([P, 4, P], BF16, tag="tp", name=name + "_ps")
                for m in range(4):
                    nc.tensor.transpose(tt[:, m, :], table[:, m, :], ident_bf[:])
                sb = keep.tile([P, 4, P], BF16, name=name)
                nc.scalar.copy(out=sb[:], in_=tt[:])
                turned.append(sb)
            lo, hi = slice(0, HALF), slice(HALF, P)
            for kind in range(2):
                for part, source, o, sign in ((lo, 0, 0, 0), (hi, 0, 1, 0), (lo, 1, 1, 0), (hi, 1, 0, 1)):
                    nc.scalar.activation(
                        out=diag[part, kind, source, o, :], in_=ident_bf[part, :], func=ACT.Copy,
                        scale=wcol[part, kind, sign : sign + 1],
                    )
            for kind in range(2):
                for half in range(2):
                    tb = ps_t.tile([P, 2, 2, D], F32, tag="tp", name="tab_%d_%d" % (kind, half))
                    for mm in range(2):
                        for source in range(2):
                            nc.tensor.matmul(
                                out=tb[:, mm, :, :], lhsT=turned[source][:, 2 * half + mm, :],
                                rhs=diag[:, kind, source, :, :], start=(source == 0), stop=(source == 1),
                            )
                    nc.scalar.copy(out=cf_all[:, kind, 2 * half : 2 * half + 2, :, :], in_=tb[:])

        grouped = {}
        codes = {}
        planes = {}
        acc = {}
        ssq = {}
        inv = {}
        prod = {}
        rot = {}

        def product_piece(j, t, cols):
            nc.vector.tensor_tensor(
                out=src[("q", j)][t][:, cols], in0=wq8[j][:, t, cols].bitcast(FP8), in1=scl[:, cols], op=ALU.mult
            )

        def product(j, t):
            src[("q", j)].append(rows.tile([P, HID], BF16, tag="row", name="q%d_%d" % (j, t)))
            product_piece(j, t, slice(0, HID))

        def turn(key, t, halves=(0, 1)):
            if key not in grouped:
                grouped[key] = grp.tile([P, 4, 512, 4], BF16, tag="grp", name="grp_%s%d" % key, align_bytes=64)
            words = src[key][t][:].bitcast(F32)
            gw = grouped[key][:].bitcast(F32)
            for half in halves:
                tp = ps_t.tile([P, 2, 2, P], F32, tag="tp", name="tp_%s%d_%d_%d" % (key[0], key[1], t, half))
                for gg in range(2):
                    g = 2 * half + gg
                    for u in range(2):
                        nc.tensor.transpose(tp[:, gg, u, :], words[:, 256 * g + u : 256 * (g + 1) : 2], ident[:])
                dst = gw[:, 2 * half : 2 * half + 2, t * P : (t + 1) * P, :]
                if half == 1 and key in VCOPIES:
                    nc.vector.tensor_copy(out=dst, in_=tp[:].rearrange("p g u r -> p g r u"))
                else:
                    nc.scalar.copy(out=dst, in_=tp[:].rearrange("p g u r -> p g r u"))

        def quantise(key, half):
            if half == 0:
                pool = keep if key[0] == "x" else cod
                codes[key] = pool.tile([P, 4, 512], U32, tag="codes_" + ("x" if key[0] == "x" else "w"),
                                       name="codes_%s%d" % key, align_bytes=64)
                planes[key] = pool.tile([P, 4, 512], U8, tag="planes_" + ("x" if key[0] == "x" else "w"),
                                        name="planes_%s%d" % key, align_bytes=64)
            gs = slice(2 * half, 2 * half + 2)
            nc.vector.quantize_mx(
                out=codes[key][:, gs, :].rearrange("p g c -> p (g c)").bitcast(FP8X4),
                scales=planes[key][:, gs, :].rearrange("p g c -> p (g c)"),
                in_=grouped[key][:, gs, :, :].rearrange("p g r t -> p (g r t)"),
            )

        def multiply(r, m):
            key = SEQ[r]
            a = ps_a.tile([P, 512], F32, tag="acc", name="acc_%d_%d" % (r, m))
            toks = slice(m * P, (m + 1) * P)
            for g in range(4):
                nc.tensor.matmul_mx(
                    out=a[:],
                    lhsT=codes[("x", 0)][:, g, toks].bitcast(FP8X4),
                    lhsT_scale=planes[("x", 0)][:, g, toks],
                    rhs=codes[key][:, g, :].bitcast(FP8X4),
                    rhs_scale=planes[key][:, g, :],
                    start=(g == 0),
                    stop=(g == 3),
                )
            acc[(r, m)] = a

        def squares(r, m):
            if m == 0:
                ssq[r] = stat.tile([P, 16], F32, tag="ssq", name="ssq_%d" % r)
            for h in range(4):
                junk = work.tile([P, D], F32, tag="junk", name="junk_%d_%d_%d" % (r, m, h))
                nc.scalar.activation(
                    out=junk[:], in_=acc[(r, m)][:, h * D : (h + 1) * D], func=ACT.Square,
                    accum_out=ssq[r][:, 4 * m + h : 4 * m + h + 1],
                )

        def root(r):
            inv[r] = stat.tile([P, 16], F32, tag="inv", name="inv_%d" % r)
            nc.scalar.activation(out=inv[r][:], in_=ssq[r][:], func=ACT.Abs_reciprocal_sqrt, scale=1.0 / D, bias=EPS)

        def rope_mult(r, m):
            pe = m == 2 and r in (1, 3)
            pr = work.tile([P, 4, 2, D], F32, tag="prodp" if pe else "prod", bufs=1 if pe else 4, name="prod_%d_%d" % (r, m))
            nc.vector.tensor_tensor(
                out=pr[:],
                in0=acc[(r, m)][:].rearrange("p (h d) -> p h d", h=4).unsqueeze(2).to_broadcast([P, 4, 2, D]),
                in1=cf[SEQ[r][0]][:, m, :, :].unsqueeze(1).to_broadcast([P, 4, 2, D]),
                op=ALU.mult,
            )
            prod[(r, m)] = pr

        def rope_mult_scaled(r, m):
            pe = m == 2 and r in (1, 3)
            pr = work.tile([P, 4, 2, D], F32, tag="prodp" if pe else "prod", bufs=1 if pe else 4, name="prod_%d_%d" % (r, m))
            for h in range(4):
                nc.vector.scalar_tensor_tensor(
                    out=pr[:, h, :, :],
                    in0=acc[(r, m)][:, h * D : (h + 1) * D].unsqueeze(1).to_broadcast([P, 2, D]),
                    scalar=inv[r][:, 4 * m + h : 4 * m + h + 1],
                    in1=cf[SEQ[r][0]][:, m, :, :],
                    op0=ALU.mult, op1=ALU.mult,
                )
            prod[(r, m)] = pr

        def store_only(r, m):
            key = SEQ[r]
            h0 = 4 * key[1]
            dst = outs[key[0]][0, h0 : h0 + 4, m * P : (m + 1) * P, :].rearrange("h s d -> s h d")
            nc.sync.dma_start(out=dst, in_=rot[(r, m)][:].rearrange("p h a b -> p h (a b)"))

        def rope_add(r, m, eng):
            kept = m == 3 and r < groups - 1
            ro = work.tile([P, 4, 2, HALF], F32, tag="rotl" if kept else "rot", bufs=2 if kept else 5, name="rot_%d_%d" % (r, m))
            pr = prod[(r, m)]
            eng.tensor_tensor(out=ro[:], in0=pr[:, :, :, 0:HALF], in1=pr[:, :, :, HALF:D], op=ALU.add)
            rot[(r, m)] = ro

        gate = keep.tile([P, 8], U32, name="gate")

        def wait_for_quantise(key):
            nc.gpsimd.tensor_copy(out=gate[:], in_=codes[key][:, 3, 504:512])

        def pe_add(r, m):
            s = ps_t.tile([P, 512], F32, tag="tp", name="sum_%d_%d" % (r, m))
            pr = prod[(r, m)]
            for half in range(2):
                nc.tensor.matmul(
                    out=s[:].rearrange("p (h d) -> p h d", d=HALF), lhsT=ident[:],
                    rhs=pr[:, :, :, half * HALF : (half + 1) * HALF].rearrange("p h a d -> p (h a) d"),
                    start=(half == 0), stop=(half == 1),
                )
            summed[(r, m)] = s

        summed = {}

        def finish(r, m):
            key = SEQ[r]
            if key[0] != "v" and m in (3,):
                store_only(r, m)
                return
            o = work.tile([P, 4, D], F32, tag="o", bufs=6, name="o_%d_%d" % (r, m))
            for h in range(4):
                if (r, m) in summed:
                    val = summed[(r, m)][:, h * D : (h + 1) * D]
                elif key[0] == "v":
                    val = acc[(r, m)][:, h * D : (h + 1) * D]
                else:
                    val = rot[(r, m)][:, h, :, :].rearrange("p a b -> p (a b)")
                nc.scalar.activation(out=o[:, h, :], in_=val, func=ACT.Copy, scale=inv[r][:, 4 * m + h : 4 * m + h + 1])
            h0 = 4 * key[1]
            dst = outs[key[0]][0, h0 : h0 + 4, m * P : (m + 1) * P, :].rearrange("h s d -> s h d")
            nc.sync.dma_start(out=dst, in_=o[:])

        left = []
        late = []
        for r in range(-2, groups + 1):
            live = 0 <= r < groups
            is_v = live and SEQ[r][0] == "v"
            if r == -1:
                tables()
            if r == -2:
                for t in range(4):
                    src[("q", 0)].append(rows.tile([P, HID], BF16, tag="row", name="q0_%d" % t))
                for half in range(2):
                    for c in (2 * half, 2 * half + 1):
                        for t in range(4):
                            product_piece(0, t, slice(512 * c, 512 * (c + 1)))
                    for t in ((0,), (1, 2, 3))[half]:
                        turn(("x", 0), t)
                    for t in range(4):
                        turn(("q", 0), t, (half,))
            if r - 2 in (1, 3):
                pe_add(r - 2, 2)
                finish(r - 2, 2)
            for m in range(4 if r > -2 else 0):
                if live:
                    multiply(r, m)
                    squares(r, m)
                    if m == 3:
                        root(r)
                if r == groups and m >= 2:
                    if m == 2:
                        store_only(r - 1, 3)
                        finish(r - 1, 2)
                elif 1 <= r and SEQ[r - 1][0] != "v" and not (m == 3 and r - 1 < groups - 1) and not (m == 2 and r - 1 in (1, 3)):
                    finish(r - 1, m)
                if m == (0 if r == groups else 3) and late:
                    finish(late.pop(), 3)
                for jt in PRODUCTS.get((r, m), ()):
                    product(jt[0], jt[1])
                if r == -2:
                    turn(("x", 0), m)
                if 0 <= r + 2 < groups:
                    turn(SEQ[r + 2], m)
            if is_v:
                for m in range(4):
                    finish(r, m)
            if r == -1:
                quantise(("x", 0), 0)
                quantise(("x", 0), 1)
            if 0 <= r + 1 < groups:
                quantise(SEQ[r + 1], 0)
                quantise(SEQ[r + 1], 1)
            if live and not is_v:
                last = r == groups - 1
                if left:
                    if not last:
                        wait_for_quantise(SEQ[r + 1])
                    rope_add(left[0], 3, nc.gpsimd)
                    late.append(left.pop())
                for m in range(4):
                    if m in (3,) or (last and m == 3):
                        rope_mult_scaled(r, m)
                    else:
                        rope_mult(r, m)
                    if m >= 1 and m - 1 < GADDS:
                        rope_add(r, m - 1, nc.gpsimd)
                if r not in (1, 3):
                    rope_add(r, 2, nc.vector)
                if last:
                    rope_add(r, 3, nc.vector)
                else:
                    left.append(r)
